import numpy as np
import ml_dtypes


def mxq(x, axis, fmt="e4m3"):
    dtype, down = {"e4m3": (ml_dtypes.float8_e4m3fn, 7), "e5m2": (ml_dtypes.float8_e5m2, 14)}[fmt]
    v = np.moveaxis(np.asarray(x, np.float32).astype(ml_dtypes.bfloat16).astype(np.float64), axis, -1)
    blocks = v.reshape(v.shape[:-1] + (-1, 32))
    amax = np.abs(blocks).max(-1, keepdims=True)
    byte = np.maximum(np.where(amax > 0, np.frexp(amax)[1] - 1 + 127, 0) - down, 1)
    scale = np.exp2(byte - 127.0)
    codes = (blocks / scale).astype(np.float32).astype(dtype).astype(np.float64)
    return np.moveaxis((codes * scale).reshape(v.shape), -1, axis)


WIDE = False


def mx_kscale(k):
    if not WIDE:
        return np.ones(k)
    levels = np.array([10, -10, 5, -5, 0])
    if k % 512:
        return np.exp2(np.random.permutation(np.resize(levels, k // 32))).repeat(32)
    a = np.empty((k // 512, 16))
    for p in range(k // 512):
        a[p, :8] = np.random.permutation(np.resize(levels, 8))
        for g in range(8):
            far = levels[np.abs(levels - a[p, g]) >= 10]
            a[p, g + 8] = far[np.random.randint(len(far))]
    return np.exp2(a.ravel()).repeat(32)


BF16 = ml_dtypes.bfloat16


def bf(x):
    return np.asarray(x, np.float32).astype(BF16)


def f64(x):
    return np.asarray(x).astype(np.float64)


E, T, G, C = 256, 3, 3, 1024


def silu(v):
    return v / (1.0 + np.exp(-v))


def setup_inputs():
    n = np.random.standard_normal
    s = mx_kscale(C)
    t = mx_kscale(G * C).reshape(G, C)
    r = np.sqrt(C)
    return {
        "edge": bf(n((E, C)) * s),
        "edge_nei_len": bf(n((E, T, C)) * s),
        "edge_nei_angle": bf(n((E, T, C)) * s),
        "Wk": bf(n((C, C)) / r / s[:, None] * t[0]),
        "bk": bf(n(C) * 0.2 * t[0]),
        "Wke": bf(n((T, C, C)) / r / s[:, None] * t[1]),
        "bke": bf(n((T, C)) * 0.2 * t[1]),
        "We": bf(n((C, C)) / r / s[:, None] * t[2]),
        "Wk1": bf(n((G * C, C)) / np.sqrt(G * C) / t.reshape(G * C, 1)),
        "bk1": bf(n(C) * 0.2),
    }


def reference(edge, edge_nei_len, edge_nei_angle, Wk, bk, Wke, bke, We, Wk1, bk1):
    kx = (mxq(f64(edge), 1, "e4m3") @ mxq(f64(Wk), 0, "e4m3")) + f64(bk)
    ky = (mxq(f64(edge_nei_len).transpose(1, 0, 2), 2, "e4m3") @ mxq(f64(Wke), 1, "e4m3")) + f64(bke)[:, None, :]
    ky = ky.transpose(1, 0, 2)
    exy = mxq(f64(edge_nei_angle), 2, "e4m3") @ mxq(f64(We), 0, "e4m3")
    w_x, w_y, w_e = f64(Wk1).reshape(G, C, C)
    pre = ((mxq(kx, 1, "e4m3") @ mxq(w_x, 0, "e4m3"))[:, None, :]
           + (mxq(ky, 2, "e4m3") @ mxq(w_y, 0, "e4m3"))
           + (mxq(exy, 2, "e4m3") @ mxq(w_e, 0, "e4m3"))
           + f64(bk1))
    return silu(pre)

@@ -1,0 +1,332 @@
+from contextlib import ExitStack
+
+import concourse.mybir as mybir
+from concourse.masks import make_identity
+
+F32 = mybir.dt.float32
+BF16 = mybir.dt.bfloat16
+U32 = mybir.dt.uint32
+U8 = mybir.dt.uint8
+FP8X4 = mybir.dt.float8_e4m3fn_x4
+ADD = mybir.AluOpType.add
+SILU = mybir.ActivationFunctionType.Silu
+
+P = 128
+PACK = 4
+K_PASS = P * PACK
+BANK = 512
+
+E = 256
+T = 3
+C = 1024
+E_BLOCKS = E // P
+PASSES = C // K_PASS
+STREAMS = 3
+UNITS = 1 + T + T
+HALF = BANK
+RUN = 8
+VECTOR_SLOTS = 2
+SLOT_COLS = C // PACK
+FIRST_WEIGHTS = 2 + T
+FIRST_CHUNKS = FIRST_WEIGHTS * PASSES
+SECOND_ORDER = (0, 2, 1)
+RAW_BUFS = 4
+
+FLOPS = 2 * 2 * UNITS * E * C * C
+
+
+def tile_comformerconvedgelayer_pa_kernel(
+    tc, edge, edge_nei_len, edge_nei_angle, Wk, bk, Wke, bke, We, Wk1, bk1, out
+):
+    nc = tc.nc
+    m_tiles = C // P
+    n_halves = C // BANK
+    with ExitStack() as ctx:
+        consts = ctx.enter_context(tc.tile_pool(name="consts", bufs=1))
+        keep = ctx.enter_context(tc.tile_pool(name="keep", bufs=1))
+        raw_pool = ctx.enter_context(tc.tile_pool(name="raw", bufs=RAW_BUFS))
+        grouped_pool = ctx.enter_context(tc.tile_pool(name="grouped", bufs=3))
+        first_w_pool = ctx.enter_context(tc.tile_pool(name="first_w", bufs=2))
+        act_pool = ctx.enter_context(tc.tile_pool(name="act", bufs=4))
+        result_pool = ctx.enter_context(tc.tile_pool(name="result", bufs=E_BLOCKS * T))
+        psum = ctx.enter_context(tc.psum_pool(name="psum", bufs=8))
+
+        bias_rows = consts.tile([P, P], BF16)
+        nc.vector.memset(bias_rows[:], 0.0)
+        for unit in range(1 + T):
+            source = bk if unit == 0 else bke[unit - 1, :]
+            for q in range(PASSES):
+                row = unit * m_tiles + q * PACK
+                nc.scalar.dma_start(
+                    out=bias_rows[row : row + PACK, :],
+                    in_=source[q * K_PASS : (q + 1) * K_PASS].rearrange("(a j b) -> j a b", j=PACK, b=RUN),
+                )
+        bk1_row = consts.tile([P, C], BF16)
+        nc.vector.memset(bk1_row[:], 0.0)
+        nc.scalar.dma_start(out=bk1_row[0:1, :], in_=bk1.rearrange("(o c) -> o c", o=1))
+        ones = consts.tile([P, P], BF16)
+        nc.vector.memset(ones[:], 1.0)
+
+        warm = consts.tile([P, 1], F32)
+        nc.vector.memset(warm[:], 0.0)
+        nc.scalar.activation(out=warm[:], in_=warm[:], func=SILU)
+
+        ident_f32 = consts.tile([P, P], F32)
+        make_identity(nc, ident_f32[:])
+        ident_bf16 = consts.tile([P, P], BF16)
+        make_identity(nc, ident_bf16[:])
+        first_bias = consts.tile([P, (1 + T) * m_tiles], F32)
+        bk1_all = consts.tile([P, C], F32)
+
+        x_words = keep.tile([P, UNITS, PASSES * E], U32, align_bytes=64)
+        x_scales = keep.tile([P, UNITS, PASSES * E], U8, align_bytes=64)
+        h_words = keep.tile([P, UNITS, PASSES * E], U32, align_bytes=64)
+        h_scales = keep.tile([P, UNITS, PASSES * E], U8, align_bytes=64)
+        w2_words = keep.tile([P, n_halves, STREAMS * PASSES, BANK], U32, align_bytes=64)
+        w2_scales = keep.tile([P, n_halves, STREAMS * PASSES, BANK], U8, align_bytes=64)
+        we_words = keep.tile([P, PASSES, C], U32, align_bytes=64)
+        we_scales = keep.tile([P, PASSES, C], U8, align_bytes=64)
+        w1_words = {0: we_words}
+        w1_scales = {0: we_scales}
+
+        chunks = []
+        regrouped = {}
+        first_weights = (We, Wk, Wke[0], Wke[1], Wke[2])
+        n_chunks = FIRST_CHUNKS + n_halves * STREAMS
+
+        def load_next_chunk():
+            index = len(chunks)
+            if index == n_chunks:
+                return
+            raw = raw_pool.tile([P, PACK, C], BF16)
+            if index < FIRST_CHUNKS:
+                weight, g = divmod(index, PASSES)
+                rows = first_weights[weight][g * K_PASS : (g + 1) * K_PASS, :]
+                nc.sync.dma_start(out=raw[:], in_=rows.rearrange("(p t) c -> p t c", t=PACK))
+            else:
+                h, position = divmod(index - FIRST_CHUNKS, STREAMS)
+                for q in range(PASSES):
+                    top = (SECOND_ORDER[position] * PASSES + q) * K_PASS
+                    rows = Wk1[top : top + K_PASS, h * BANK : (h + 1) * BANK].rearrange(
+                        "(a j b) n -> j a b n", j=PACK, b=RUN
+                    )
+                    for j in range(PACK):
+                        nc.sync.dma_start(out=raw[:, j, q * HALF : (q + 1) * HALF], in_=rows[j])
+            chunks.append(raw)
+
+        def regroup(index):
+            grouped = grouped_pool.tile([P, C, PACK], BF16, align_bytes=64)
+            if index < FIRST_CHUNKS:
+                for j in range(PACK):
+                    copy = nc.vector.tensor_copy if j < VECTOR_SLOTS else nc.scalar.copy
+                    copy(
+                        out=grouped[:, j * SLOT_COLS : (j + 1) * SLOT_COLS, :].rearrange("p (x b) t -> p x t b", b=RUN),
+                        in_=chunks[index][:].rearrange("p t (x j b) -> p j x t b", j=PACK, b=RUN)[:, j],
+                    )
+            else:
+                for copy, cols in ((nc.vector.tensor_copy, slice(0, HALF)), (nc.scalar.copy, slice(HALF, C))):
+                    copy(
+                        out=grouped[:, cols, :].rearrange("p (x b) t -> p x t b", b=RUN),
+                        in_=chunks[index][:, :, cols].rearrange("p t (x b) -> p x t b", b=RUN),
+                    )
+            regrouped[index] = grouped
+            load_next_chunk()
+
+        def quantise_chunk(index):
+            for half in range(2):
+                cols = slice(half * HALF, (half + 1) * HALF)
+                if index < FIRST_CHUNKS:
+                    weight, g = divmod(index, PASSES)
+                    words, scales = w1_words[weight][:, g, cols], w1_scales[weight][:, g, cols]
+                else:
+                    h, position = divmod(index - FIRST_CHUNKS, STREAMS)
+                    q = SECOND_ORDER[position] * PASSES + half
+                    words, scales = w2_words[:, h, q, :], w2_scales[:, h, q, :]
+                nc.vector.quantize_mx(
+                    out=words.bitcast(FP8X4),
+                    scales=scales,
+                    in_=regrouped[index][:, cols, :].rearrange("p c t -> p (c t)"),
+                )
+
+        x_rows = {}
+        x_grouped = {}
+
+        def load_activations(unit):
+            if unit == 0:
+                source = edge
+            elif unit <= T:
+                source = edge_nei_len[:, unit - 1, :]
+            else:
+                source = edge_nei_angle[:, unit - 1 - T, :]
+            x_rows[unit] = keep.tile([P, E_BLOCKS, C], BF16, name="x_rows%d" % unit)
+            nc.sync.dma_start(out=x_rows[unit][:], in_=source.rearrange("(b p) k -> p b k", p=P))
+
+        def transpose_activations(unit):
+            grouped = act_pool.tile([P, PASSES * E * PACK], BF16, align_bytes=64, tag="x_grouped")
+            grouped_pairs = grouped[:].bitcast(F32).rearrange("p (g r u) -> p g r u", g=PASSES, u=2)
+            for b in range(E_BLOCKS):
+                pairs = x_rows[unit][:, b, :].bitcast(F32)
+                turned = psum.tile([P, BANK], F32, tag="bank")
+                for w in range(BANK // P):
+                    g, u = divmod(w, 2)
+                    nc.tensor.transpose(
+                        turned[:, w * P : (w + 1) * P], pairs[:, g * 2 * P + u : (g + 1) * 2 * P : 2], ident_f32[:]
+                    )
+                nc.scalar.copy(
+                    out=grouped_pairs[:, :, b * P : (b + 1) * P, :],
+                    in_=turned[:].rearrange("p (g u r) -> p g r u", g=PASSES, u=2),
+                )
+            x_grouped[unit] = grouped
+
+        def quantise_activations(unit):
+            nc.vector.quantize_mx(
+                out=x_words[:, unit, :].bitcast(FP8X4),
+                scales=x_scales[:, unit, :],
+                in_=x_grouped[unit][:],
+            )
+
+        first_accs = {}
+        h_grouped = {}
+
+        def first_passes(unit):
+            weight = 1 + unit if unit <= T else 0
+            words, scales = w1_words[weight], w1_scales[weight]
+            first_accs[unit] = []
+            for q in range(PASSES):
+                for b in range(E_BLOCKS):
+                    acc = psum.tile([P, BANK], F32, tag="bank")
+                    for j in range(PACK):
+                        m_cols = slice(j * SLOT_COLS + q * P, j * SLOT_COLS + (q + 1) * P)
+                        for g in range(PASSES):
+                            e_cols = slice(g * E + b * P, g * E + (b + 1) * P)
+                            nc.tensor.matmul_mx(
+                                out=acc[:, j * P : (j + 1) * P],
+                                lhsT=words[:, g, m_cols].bitcast(FP8X4),
+                                lhsT_scale=scales[:, g, m_cols],
+                                rhs=x_words[:, unit, e_cols].bitcast(FP8X4),
+                                rhs_scale=x_scales[:, unit, e_cols],
+                                start=(g == 0),
+                                stop=(g == PASSES - 1),
+                            )
+                    first_accs[unit].append(acc)
+
+        def first_out(unit):
+            grouped = act_pool.tile([P, PASSES * E_BLOCKS, P, PACK], BF16, align_bytes=64, tag="h_grouped", bufs=3)
+            for a, acc in enumerate(first_accs[unit]):
+                interleaved = acc[:].rearrange("p (j r) -> p r j", j=PACK)
+                if unit > T:
+                    nc.scalar.copy(out=grouped[:, a], in_=interleaved)
+                else:
+                    first = unit * m_tiles + (a // E_BLOCKS) * PACK
+                    nc.vector.tensor_tensor(
+                        out=grouped[:, a],
+                        in0=interleaved,
+                        in1=first_bias[:, first : first + PACK].unsqueeze(1).to_broadcast([P, P, PACK]),
+                        op=ADD,
+                    )
+            h_grouped[unit] = grouped
+
+        def quantise_hidden(unit):
+            nc.vector.quantize_mx(
+                out=h_words[:, unit, :].bitcast(FP8X4),
+                scales=h_scales[:, unit, :],
+                in_=h_grouped[unit][:].rearrange("p a r j -> p (a r j)"),
+            )
+
+        def second_passes(index, accs):
+            h, position = divmod(index - FIRST_CHUNKS, STREAMS)
+            s = SECOND_ORDER[position]
+            for b in range(E_BLOCKS):
+                for t in range(T):
+                    for q in range(PASSES):
+                        unit = 0 if s == 0 else 1 + (s - 1) * T + t
+                        e_cols = slice((q * E_BLOCKS + b) * P, (q * E_BLOCKS + b + 1) * P)
+                        nc.tensor.matmul_mx(
+                            out=accs[b * T + t][:],
+                            lhsT=h_words[:, unit, e_cols].bitcast(FP8X4),
+                            lhsT_scale=h_scales[:, unit, e_cols],
+                            rhs=w2_words[:, h, s * PASSES + q, :].bitcast(FP8X4),
+                            rhs_scale=w2_scales[:, h, s * PASSES + q, :],
+                            start=(position == 0 and q == 0),
+                            stop=(position == STREAMS - 1 and q == PASSES - 1),
+                        )
+
+        def open_banks():
+            return [psum.tile([P, BANK], F32, tag="bank", name="acc2") for i in range(E_BLOCKS * T)]
+
+        def finish(h, accs):
+            n_cols = slice(h * BANK, (h + 1) * BANK)
+            for b in range(E_BLOCKS):
+                for t in range(T):
+                    result = result_pool.tile([P, BANK], F32)
+                    nc.vector.tensor_tensor(
+                        out=result[:], in0=accs[b * T + t][:], in1=bk1_all[:, n_cols], op=ADD
+                    )
+                    nc.scalar.activation(out=result[:], in_=result[:], func=SILU)
+                    nc.sync.dma_start(out=out[b * P : (b + 1) * P, t, n_cols], in_=result[:])
+
+        load_next_chunk()
+        load_next_chunk()
+        for t in range(T):
+            load_activations(1 + T + t)
+        load_activations(0)
+        load_next_chunk()
+
+        for phase in range(FIRST_WEIGHTS + 1):
+            arriving = phase - 1
+            complete = phase - 2
+            exy_out = T + phase - 1
+            if 1 <= phase < FIRST_WEIGHTS:
+                w1_words[phase] = first_w_pool.tile([P, PASSES, C], U32, align_bytes=64, name="w1_words")
+                w1_scales[phase] = first_w_pool.tile([P, PASSES, C], U8, align_bytes=64, name="w1_scales")
+
+            regroup(2 * phase)
+            if phase < T:
+                load_activations(1 + phase)
+            if phase > 0:
+                quantise_chunk(2 * phase - 1)
+            if phase == 1:
+                for t in range(T):
+                    transpose_activations(1 + T + t)
+                bias_cols = psum.tile([P, P], BF16, tag="bank")
+                nc.tensor.transpose(bias_cols[:], bias_rows[:], ident_bf16[:])
+                nc.vector.tensor_copy(out=first_bias[:], in_=bias_cols[:, 0 : (1 + T) * m_tiles])
+            if 0 <= arriving <= T:
+                transpose_activations(arriving)
+            if complete >= 0:
+                first_passes(complete)
+            if 2 <= phase <= 1 + T:
+                first_out(exy_out)
+
+            regroup(2 * phase + 1)
+            quantise_chunk(2 * phase)
+            if phase == 1:
+                for t in range(T):
+                    quantise_activations(1 + T + t)
+            if 0 <= arriving <= T:
+                quantise_activations(arriving)
+            if complete >= 0:
+                first_out(complete)
+                quantise_hidden(complete)
+            if 2 <= phase <= 1 + T:
+                quantise_hidden(exy_out)
+            if 1 <= phase <= T:
+                first_passes(T + phase)
+
+        for h in range(n_halves):
+            cols = slice(h * BANK, (h + 1) * BANK)
+            spread = psum.tile([P, BANK], F32, tag="bank")
+            nc.tensor.matmul(out=spread[:], lhsT=ones[:], rhs=bk1_row[:, cols], start=True, stop=True)
+            nc.vector.tensor_copy(out=bk1_all[:, cols], in_=spread[:])
+
+        accs = open_banks()
+        second_passes(FIRST_CHUNKS, accs)
+        for index in range(FIRST_CHUNKS + 2, n_chunks + 1):
+            if index < n_chunks:
+                regroup(index)
+            quantise_chunk(index - 1)
+            if index - 1 == FIRST_CHUNKS + STREAMS:
+                finish(0, accs)
+                accs = open_banks()
+            second_passes(index - 1, accs)
+        finish(1, accs)

@@ -9,6 +9,7 @@ U32 = mybir.dt.uint32
 U8 = mybir.dt.uint8
 FP8X4 = mybir.dt.float8_e4m3fn_x4
 ADD = mybir.AluOpType.add
+MULT = mybir.AluOpType.mult
 SILU = mybir.ActivationFunctionType.Silu
 
 P = 128
@@ -25,8 +26,10 @@ STREAMS = 3
 UNITS = 1 + T + T
 HALF = BANK
 RUN = 8
-VECTOR_SLOTS = 2
 SLOT_COLS = C // PACK
+VECTOR_TILES = 4
+VECTOR_TILES_WKE = 3
+VECTOR_COLS = 448
 FIRST_WEIGHTS = 2 + T
 FIRST_CHUNKS = FIRST_WEIGHTS * PASSES
 SECOND_ORDER = (0, 2, 1)
@@ -39,7 +42,7 @@ def tile_comformerconvedgelayer_pa_kernel(
     tc, edge, edge_nei_len, edge_nei_angle, Wk, bk, Wke, bke, We, Wk1, bk1, out
 ):
     nc = tc.nc
-    m_tiles = C // P
+    n_bias_rows = (1 + T) * PASSES
     n_halves = C // BANK
     with ExitStack() as ctx:
         consts = ctx.enter_context(tc.tile_pool(name="consts", bufs=1))
@@ -51,31 +54,36 @@ def tile_comformerconvedgelayer_pa_kernel(
         result_pool = ctx.enter_context(tc.tile_pool(name="result", bufs=E_BLOCKS * T))
         psum = ctx.enter_context(tc.psum_pool(name="psum", bufs=8))
 
-        bias_rows = consts.tile([P, P], BF16)
-        nc.vector.memset(bias_rows[:], 0.0)
-        for unit in range(1 + T):
-            source = bk if unit == 0 else bke[unit - 1, :]
-            for q in range(PASSES):
-                row = unit * m_tiles + q * PACK
-                nc.scalar.dma_start(
-                    out=bias_rows[row : row + PACK, :],
-                    in_=source[q * K_PASS : (q + 1) * K_PASS].rearrange("(a j b) -> j a b", j=PACK, b=RUN),
-                )
+        warm = consts.tile([P, 1], F32)
+        nc.vector.memset(warm[:], 0.0)
+        nc.scalar.activation(out=warm[:], in_=warm[:], func=SILU)
+
+        bias_rows = consts.tile([n_bias_rows, K_PASS], BF16)
+        nc.scalar.dma_start(out=bias_rows[0:PASSES, :], in_=bk.rearrange("(q c) -> q c", q=PASSES))
+        nc.scalar.dma_start(
+            out=bias_rows[PASSES:n_bias_rows, :], in_=bke.rearrange("t (q c) -> (t q) c", q=PASSES)
+        )
+        sorted_bias = consts.tile([P, PACK, P], BF16)
+        nc.gpsimd.memset(sorted_bias[:], 0.0)
+        nc.gpsimd.tensor_scalar(
+            out=sorted_bias[0:n_bias_rows, :, :].rearrange("r j (a b) -> r j a b", b=RUN),
+            in0=bias_rows[:].rearrange("r (a j b) -> r j a b", j=PACK, b=RUN),
+            scalar1=1.0,
+            scalar2=0.0,
+            op0=MULT,
+            op1=ADD,
+        )
         bk1_row = consts.tile([P, C], BF16)
         nc.vector.memset(bk1_row[:], 0.0)
         nc.scalar.dma_start(out=bk1_row[0:1, :], in_=bk1.rearrange("(o c) -> o c", o=1))
         ones = consts.tile([P, P], BF16)
         nc.vector.memset(ones[:], 1.0)
 
-        warm = consts.tile([P, 1], F32)
-        nc.vector.memset(warm[:], 0.0)
-        nc.scalar.activation(out=warm[:], in_=warm[:], func=SILU)
-
         ident_f32 = consts.tile([P, P], F32)
         make_identity(nc, ident_f32[:])
         ident_bf16 = consts.tile([P, P], BF16)
         make_identity(nc, ident_bf16[:])
-        first_bias = consts.tile([P, (1 + T) * m_tiles], F32)
+        first_bias = consts.tile([P, n_bias_rows, PACK], F32)
         bk1_all = consts.tile([P, C], F32)
 
         x_words = keep.tile([P, UNITS, PASSES * E], U32, align_bytes=64)
@@ -101,8 +109,10 @@ def tile_comformerconvedgelayer_pa_kernel(
             raw = raw_pool.tile([P, PACK, C], BF16)
             if index < FIRST_CHUNKS:
                 weight, g = divmod(index, PASSES)
-                rows = first_weights[weight][g * K_PASS : (g + 1) * K_PASS, :]
-                nc.sync.dma_start(out=raw[:], in_=rows.rearrange("(p t) c -> p t c", t=PACK))
+                rows = first_weights[weight][g * K_PASS : (g + 1) * K_PASS, :].rearrange("(p t) c -> p t c", t=PACK)
+                width = HALF if index == 0 else C
+                for left in range(0, C, width):
+                    nc.sync.dma_start(out=raw[:, :, left : left + width], in_=rows[:, :, left : left + width])
             else:
                 h, position = divmod(index - FIRST_CHUNKS, STREAMS)
                 for q in range(PASSES):
@@ -117,14 +127,27 @@ def tile_comformerconvedgelayer_pa_kernel(
         def regroup(index):
             grouped = grouped_pool.tile([P, C, PACK], BF16, align_bytes=64)
             if index < FIRST_CHUNKS:
-                for j in range(PACK):
-                    copy = nc.vector.tensor_copy if j < VECTOR_SLOTS else nc.scalar.copy
-                    copy(
-                        out=grouped[:, j * SLOT_COLS : (j + 1) * SLOT_COLS, :].rearrange("p (x b) t -> p x t b", b=RUN),
-                        in_=chunks[index][:].rearrange("p t (x j b) -> p j x t b", j=PACK, b=RUN)[:, j],
-                    )
+                v_tiles = VECTOR_TILES if index // PASSES < FIRST_WEIGHTS - T else VECTOR_TILES_WKE
+                pieces = [(0, PASSES)] if index > 0 else [(q, q + 1) for q in range(PASSES)]
+                for first, last in pieces:
+                    for j in range(PACK):
+                        to = grouped[:, j * SLOT_COLS : (j + 1) * SLOT_COLS, :].rearrange("p (x b) t -> p x t b", b=RUN)
+                        source = chunks[index][:].rearrange("p t (x j b) -> p j x t b", j=PACK, b=RUN)[:, j]
+                        cut = min(max(v_tiles - j * PASSES, first), last)
+                        v_runs = slice(first * P // RUN, cut * P // RUN)
+                        s_runs = slice(cut * P // RUN, last * P // RUN)
+                        if cut > first:
+                            nc.vector.tensor_copy(out=to[:, v_runs], in_=source[:, v_runs])
+                        if cut < last:
+                            nc.scalar.copy(out=to[:, s_runs], in_=source[:, s_runs])
             else:
-                for copy, cols in ((nc.vector.tensor_copy, slice(0, HALF)), (nc.scalar.copy, slice(HALF, C))):
+                pieces = [(0, C)] if index < n_chunks - 1 else [(q * HALF, (q + 1) * HALF) for q in range(PASSES)]
+                shares = []
+                for left, right in pieces:
+                    cut = left + (right - left) * VECTOR_COLS // C
+                    shares.append((nc.vector.tensor_copy, slice(left, cut)))
+                    shares.append((nc.scalar.copy, slice(cut, right)))
+                for copy, cols in shares:
                     copy(
                         out=grouped[:, cols, :].rearrange("p (x b) t -> p x t b", b=RUN),
                         in_=chunks[index][:, :, cols].rearrange("p t (x b) -> p x t b", b=RUN),
@@ -132,8 +155,8 @@ def tile_comformerconvedgelayer_pa_kernel(
             regrouped[index] = grouped
             load_next_chunk()
 
-        def quantise_chunk(index):
-            for half in range(2):
+        def quantise_chunk(index, halves=(0, 1)):
+            for half in halves:
                 cols = slice(half * HALF, (half + 1) * HALF)
                 if index < FIRST_CHUNKS:
                     weight, g = divmod(index, PASSES)
@@ -217,11 +240,11 @@ def tile_comformerconvedgelayer_pa_kernel(
                 if unit > T:
                     nc.scalar.copy(out=grouped[:, a], in_=interleaved)
                 else:
-                    first = unit * m_tiles + (a // E_BLOCKS) * PACK
+                    bias = first_bias[:, unit * PASSES + a // E_BLOCKS, :]
                     nc.vector.tensor_tensor(
                         out=grouped[:, a],
                         in0=interleaved,
-                        in1=first_bias[:, first : first + PACK].unsqueeze(1).to_broadcast([P, P, PACK]),
+                        in1=bias.unsqueeze(1).to_broadcast([P, P, PACK]),
                         op=ADD,
                     )
             h_grouped[unit] = grouped
@@ -233,12 +256,12 @@ def tile_comformerconvedgelayer_pa_kernel(
                 in_=h_grouped[unit][:].rearrange("p a r j -> p (a r j)"),
             )
 
-        def second_passes(index, accs):
+        def second_passes(index, accs, passes=(0, 1)):
             h, position = divmod(index - FIRST_CHUNKS, STREAMS)
             s = SECOND_ORDER[position]
             for b in range(E_BLOCKS):
                 for t in range(T):
-                    for q in range(PASSES):
+                    for q in passes:
                         unit = 0 if s == 0 else 1 + (s - 1) * T + t
                         e_cols = slice((q * E_BLOCKS + b) * P, (q * E_BLOCKS + b + 1) * P)
                         nc.tensor.matmul_mx(
@@ -288,9 +311,12 @@ def tile_comformerconvedgelayer_pa_kernel(
             if phase == 1:
                 for t in range(T):
                     transpose_activations(1 + T + t)
-                bias_cols = psum.tile([P, P], BF16, tag="bank")
-                nc.tensor.transpose(bias_cols[:], bias_rows[:], ident_bf16[:])
-                nc.vector.tensor_copy(out=first_bias[:], in_=bias_cols[:, 0 : (1 + T) * m_tiles])
+                bias_cols = psum.tile([P, PACK, P], BF16, tag="bank")
+                for j in range(PACK):
+                    nc.tensor.transpose(bias_cols[:, j, :], sorted_bias[:, j, :], ident_bf16[:])
+                nc.vector.tensor_copy(
+                    out=first_bias[:], in_=bias_cols[:, :, 0:n_bias_rows].rearrange("p j r -> p r j")
+                )
             if 0 <= arriving <= T:
                 transpose_activations(arriving)
             if complete >= 0:
@@ -317,16 +343,18 @@ def tile_comformerconvedgelayer_pa_kernel(
             cols = slice(h * BANK, (h + 1) * BANK)
             spread = psum.tile([P, BANK], F32, tag="bank")
             nc.tensor.matmul(out=spread[:], lhsT=ones[:], rhs=bk1_row[:, cols], start=True, stop=True)
-            nc.vector.tensor_copy(out=bk1_all[:, cols], in_=spread[:])
+            nc.scalar.copy(out=bk1_all[:, cols], in_=spread[:])
 
         accs = open_banks()
         second_passes(FIRST_CHUNKS, accs)
-        for index in range(FIRST_CHUNKS + 2, n_chunks + 1):
-            if index < n_chunks:
-                regroup(index)
+        for index in range(FIRST_CHUNKS + 2, n_chunks):
+            regroup(index)
             quantise_chunk(index - 1)
             if index - 1 == FIRST_CHUNKS + STREAMS:
                 finish(0, accs)
                 accs = open_banks()
             second_passes(index - 1, accs)
+        for q in range(PASSES):
+            quantise_chunk(n_chunks - 1, (q,))
+            second_passes(n_chunks - 1, accs, (q,))
         finish(1, accs)

@@ -26,6 +26,7 @@ STREAMS = 3
 UNITS = 1 + T + T
 HALF = BANK
 RUN = 8
+COPY_RUN = 4
 SLOT_COLS = C // PACK
 VECTOR_TILES = 4
 VECTOR_TILES_WKE = 3
@@ -131,8 +132,12 @@ def tile_comformerconvedgelayer_pa_kernel(
                 pieces = [(0, PASSES)] if index > 0 else [(q, q + 1) for q in range(PASSES)]
                 for first, last in pieces:
                     for j in range(PACK):
-                        to = grouped[:, j * SLOT_COLS : (j + 1) * SLOT_COLS, :].rearrange("p (x b) t -> p x t b", b=RUN)
-                        source = chunks[index][:].rearrange("p t (x j b) -> p j x t b", j=PACK, b=RUN)[:, j]
+                        to = grouped[:, j * SLOT_COLS : (j + 1) * SLOT_COLS, :].rearrange(
+                            "p (x i b) t -> p x i t b", i=RUN // COPY_RUN, b=COPY_RUN
+                        )
+                        source = chunks[index][:].rearrange(
+                            "p t (x j i b) -> p j x i t b", j=PACK, i=RUN // COPY_RUN, b=COPY_RUN
+                        )[:, j]
                         cut = min(max(v_tiles - j * PASSES, first), last)
                         v_runs = slice(first * P // RUN, cut * P // RUN)
                         s_runs = slice(cut * P // RUN, last * P // RUN)
@@ -149,8 +154,8 @@ def tile_comformerconvedgelayer_pa_kernel(
                     shares.append((nc.scalar.copy, slice(cut, right)))
                 for copy, cols in shares:
                     copy(
-                        out=grouped[:, cols, :].rearrange("p (x b) t -> p x t b", b=RUN),
-                        in_=chunks[index][:, :, cols].rearrange("p t (x b) -> p x t b", b=RUN),
+                        out=grouped[:, cols, :].rearrange("p (x b) t -> p x t b", b=COPY_RUN),
+                        in_=chunks[index][:, :, cols].rearrange("p t (x b) -> p x t b", b=COPY_RUN),
                     )
             regrouped[index] = grouped
             load_next_chunk()

@@ -22,19 +22,14 @@ T = 3
 C = 1024
 E_BLOCKS = E // P
 PASSES = C // K_PASS
+HALVES = C // BANK
 STREAMS = 3
 UNITS = 1 + T + T
 HALF = BANK
-RUN = 8
-COPY_RUN = 4
-SLOT_COLS = C // PACK
-VECTOR_TILES = 4
-VECTOR_TILES_WKE = 3
-VECTOR_COLS = 448
-FIRST_WEIGHTS = 2 + T
-FIRST_CHUNKS = FIRST_WEIGHTS * PASSES
 SECOND_ORDER = (0, 2, 1)
-RAW_BUFS = 4
+COPY_RUN = 8
+VECTOR_COLS = (576, 576, 560, 560, 672, 672, 400, 400, 400, 512, 512, 320, 320, 384, 384, 256)
+RAW_BUFS = 6
 
 FLOPS = 2 * 2 * UNITS * E * C * C
 
@@ -44,15 +39,24 @@ def tile_comformerconvedgelayer_pa_kernel(
 ):
     nc = tc.nc
     n_bias_rows = (1 + T) * PASSES
-    n_halves = C // BANK
+    first_weights = (We, Wk, Wke[0], Wke[1], Wke[2])
+    weight_of_unit = (1, 2, 3, 4, 0, 0, 0)
+    order = [("first", w, g) for w in range(3) for g in range(PASSES)]
+    order += [("second", s, 0) for s in SECOND_ORDER]
+    order += [("first", 3, g) for g in range(PASSES)]
+    order += [("second", s, 1) for s in SECOND_ORDER[:-1]]
+    order += [("first", 4, g) for g in range(PASSES)]
+    order += [("second", SECOND_ORDER[-1], 1)]
+    n_chunks = len(order)
     with ExitStack() as ctx:
         consts = ctx.enter_context(tc.tile_pool(name="consts", bufs=1))
         keep = ctx.enter_context(tc.tile_pool(name="keep", bufs=1))
         raw_pool = ctx.enter_context(tc.tile_pool(name="raw", bufs=RAW_BUFS))
         grouped_pool = ctx.enter_context(tc.tile_pool(name="grouped", bufs=3))
         first_w_pool = ctx.enter_context(tc.tile_pool(name="first_w", bufs=2))
-        act_pool = ctx.enter_context(tc.tile_pool(name="act", bufs=4))
-        result_pool = ctx.enter_context(tc.tile_pool(name="result", bufs=E_BLOCKS * T))
+        x_pool = ctx.enter_context(tc.tile_pool(name="x", bufs=3))
+        act_pool = ctx.enter_context(tc.tile_pool(name="act", bufs=3))
+        result_pool = ctx.enter_context(tc.tile_pool(name="result", bufs=6))
         psum = ctx.enter_context(tc.psum_pool(name="psum", bufs=8))
 
         warm = consts.tile([P, 1], F32)
@@ -67,8 +71,8 @@ def tile_comformerconvedgelayer_pa_kernel(
         sorted_bias = consts.tile([P, PACK, P], BF16)
         nc.gpsimd.memset(sorted_bias[:], 0.0)
         nc.gpsimd.tensor_scalar(
-            out=sorted_bias[0:n_bias_rows, :, :].rearrange("r j (a b) -> r j a b", b=RUN),
-            in0=bias_rows[:].rearrange("r (a j b) -> r j a b", j=PACK, b=RUN),
+            out=sorted_bias[0:n_bias_rows, :, :],
+            in0=bias_rows[:].rearrange("r (p j) -> r j p", j=PACK),
             scalar1=1.0,
             scalar2=0.0,
             op0=MULT,
@@ -87,12 +91,10 @@ def tile_comformerconvedgelayer_pa_kernel(
         first_bias = consts.tile([P, n_bias_rows, PACK], F32)
         bk1_all = consts.tile([P, C], F32)
 
-        x_words = keep.tile([P, UNITS, PASSES * E], U32, align_bytes=64)
-        x_scales = keep.tile([P, UNITS, PASSES * E], U8, align_bytes=64)
         h_words = keep.tile([P, UNITS, PASSES * E], U32, align_bytes=64)
         h_scales = keep.tile([P, UNITS, PASSES * E], U8, align_bytes=64)
-        w2_words = keep.tile([P, n_halves, STREAMS * PASSES, BANK], U32, align_bytes=64)
-        w2_scales = keep.tile([P, n_halves, STREAMS * PASSES, BANK], U8, align_bytes=64)
+        w2_words = keep.tile([P, HALVES, STREAMS * PASSES, BANK], U32, align_bytes=64)
+        w2_scales = keep.tile([P, HALVES, STREAMS * PASSES, BANK], U8, align_bytes=64)
         we_words = keep.tile([P, PASSES, C], U32, align_bytes=64)
         we_scales = keep.tile([P, PASSES, C], U8, align_bytes=64)
         w1_words = {0: we_words}
@@ -100,76 +102,63 @@ def tile_comformerconvedgelayer_pa_kernel(
 
         chunks = []
         regrouped = {}
-        first_weights = (We, Wk, Wke[0], Wke[1], Wke[2])
-        n_chunks = FIRST_CHUNKS + n_halves * STREAMS
 
-        def load_next_chunk():
+        def load_chunk():
             index = len(chunks)
-            if index == n_chunks:
-                return
-            raw = raw_pool.tile([P, PACK, C], BF16)
-            if index < FIRST_CHUNKS:
-                weight, g = divmod(index, PASSES)
-                rows = first_weights[weight][g * K_PASS : (g + 1) * K_PASS, :].rearrange("(p t) c -> p t c", t=PACK)
-                width = HALF if index == 0 else C
-                for left in range(0, C, width):
-                    nc.sync.dma_start(out=raw[:, :, left : left + width], in_=rows[:, :, left : left + width])
+            kind, which, part = order[index]
+            if index == 0:
+                halves = [
+                    consts.tile([P, PACK, HALF], BF16, name="raw_left")[:],
+                    consts.tile([P, PACK, HALF], BF16, name="raw_right")[:],
+                ]
             else:
-                h, position = divmod(index - FIRST_CHUNKS, STREAMS)
+                raw = raw_pool.tile([P, PACK, C], BF16)
+                halves = [raw[:, :, 0:HALF], raw[:, :, HALF:C]]
+            if kind == "first":
+                rows = first_weights[which][part * K_PASS : (part + 1) * K_PASS, :].rearrange("(p t) c -> p t c", t=PACK)
+                if index == 0:
+                    nc.sync.dma_start(out=halves[0], in_=rows[:, :, 0:HALF])
+                    nc.sync.dma_start(out=halves[1], in_=rows[:, :, HALF:C])
+                else:
+                    nc.sync.dma_start(out=raw[:], in_=rows)
+            else:
                 for q in range(PASSES):
-                    top = (SECOND_ORDER[position] * PASSES + q) * K_PASS
-                    rows = Wk1[top : top + K_PASS, h * BANK : (h + 1) * BANK].rearrange(
-                        "(a j b) n -> j a b n", j=PACK, b=RUN
-                    )
-                    for j in range(PACK):
-                        nc.sync.dma_start(out=raw[:, j, q * HALF : (q + 1) * HALF], in_=rows[j])
-            chunks.append(raw)
+                    top = (which * PASSES + q) * K_PASS
+                    rows = Wk1[top : top + K_PASS, part * BANK : (part + 1) * BANK]
+                    nc.sync.dma_start(out=halves[q], in_=rows.rearrange("(p t) n -> p t n", t=PACK))
+            chunks.append(halves)
 
         def regroup(index):
+            kind = order[index][0]
             grouped = grouped_pool.tile([P, C, PACK], BF16, align_bytes=64)
-            if index < FIRST_CHUNKS:
-                v_tiles = VECTOR_TILES if index // PASSES < FIRST_WEIGHTS - T else VECTOR_TILES_WKE
-                pieces = [(0, PASSES)] if index > 0 else [(q, q + 1) for q in range(PASSES)]
-                for first, last in pieces:
-                    for j in range(PACK):
-                        to = grouped[:, j * SLOT_COLS : (j + 1) * SLOT_COLS, :].rearrange(
-                            "p (x i b) t -> p x i t b", i=RUN // COPY_RUN, b=COPY_RUN
-                        )
-                        source = chunks[index][:].rearrange(
-                            "p t (x j i b) -> p j x i t b", j=PACK, i=RUN // COPY_RUN, b=COPY_RUN
-                        )[:, j]
-                        cut = min(max(v_tiles - j * PASSES, first), last)
-                        v_runs = slice(first * P // RUN, cut * P // RUN)
-                        s_runs = slice(cut * P // RUN, last * P // RUN)
-                        if cut > first:
-                            nc.vector.tensor_copy(out=to[:, v_runs], in_=source[:, v_runs])
-                        if cut < last:
-                            nc.scalar.copy(out=to[:, s_runs], in_=source[:, s_runs])
-            else:
-                pieces = [(0, C)] if index < n_chunks - 1 else [(q * HALF, (q + 1) * HALF) for q in range(PASSES)]
-                shares = []
-                for left, right in pieces:
-                    cut = left + (right - left) * VECTOR_COLS // C
-                    shares.append((nc.vector.tensor_copy, slice(left, cut)))
-                    shares.append((nc.scalar.copy, slice(cut, right)))
-                for copy, cols in shares:
-                    copy(
-                        out=grouped[:, cols, :].rearrange("p (x b) t -> p x t b", b=COPY_RUN),
-                        in_=chunks[index][:, :, cols].rearrange("p t (x b) -> p x t b", b=COPY_RUN),
-                    )
+            v_cols = VECTOR_COLS[index]
+            for q in range(PASSES):
+                to = grouped[:, q * HALF : (q + 1) * HALF, :]
+                source = chunks[index][q]
+                cut = v_cols // 2 if index in (0, n_chunks - 1) else min(max(v_cols - q * HALF, 0), HALF)
+                if kind == "first":
+                    to = to.rearrange("p (j m) t -> p m t j", j=PACK)
+                    source = source.rearrange("p t (m j) -> p m t j", j=PACK)
+                    cut = cut // PACK
+                else:
+                    to = to.rearrange("p (x b) t -> p x t b", b=COPY_RUN)
+                    source = source.rearrange("p t (x b) -> p x t b", b=COPY_RUN)
+                    cut = cut // COPY_RUN
+                if cut > 0:
+                    nc.vector.tensor_copy(out=to[:, 0:cut], in_=source[:, 0:cut])
+                if cut < to.shape[1]:
+                    nc.scalar.copy(out=to[:, cut:], in_=source[:, cut:])
             regrouped[index] = grouped
-            load_next_chunk()
 
         def quantise_chunk(index, halves=(0, 1)):
+            kind, which, part = order[index]
             for half in halves:
                 cols = slice(half * HALF, (half + 1) * HALF)
-                if index < FIRST_CHUNKS:
-                    weight, g = divmod(index, PASSES)
-                    words, scales = w1_words[weight][:, g, cols], w1_scales[weight][:, g, cols]
+                if kind == "first":
+                    words, scales = w1_words[which][:, part, cols], w1_scales[which][:, part, cols]
                 else:
-                    h, position = divmod(index - FIRST_CHUNKS, STREAMS)
-                    q = SECOND_ORDER[position] * PASSES + half
-                    words, scales = w2_words[:, h, q, :], w2_scales[:, h, q, :]
+                    row = which * PASSES + half
+                    words, scales = w2_words[:, part, row, :], w2_scales[:, part, row, :]
                 nc.vector.quantize_mx(
                     out=words.bitcast(FP8X4),
                     scales=scales,
@@ -178,6 +167,8 @@ def tile_comformerconvedgelayer_pa_kernel(
 
         x_rows = {}
         x_grouped = {}
+        x_words = {}
+        x_scales = {}
 
         def load_activations(unit):
             if unit == 0:
@@ -186,8 +177,9 @@ def tile_comformerconvedgelayer_pa_kernel(
                 source = edge_nei_len[:, unit - 1, :]
             else:
                 source = edge_nei_angle[:, unit - 1 - T, :]
-            x_rows[unit] = keep.tile([P, E_BLOCKS, C], BF16, name="x_rows%d" % unit)
-            nc.sync.dma_start(out=x_rows[unit][:], in_=source.rearrange("(b p) k -> p b k", p=P))
+            rows = x_pool.tile([P, E_BLOCKS, C], BF16, tag="x_rows", bufs=4)
+            nc.sync.dma_start(out=rows[:], in_=source.rearrange("(b p) k -> p b k", p=P))
+            x_rows[unit] = rows
 
         def transpose_activations(unit):
             grouped = act_pool.tile([P, PASSES * E * PACK], BF16, align_bytes=64, tag="x_grouped")
@@ -207,159 +199,228 @@ def tile_comformerconvedgelayer_pa_kernel(
             x_grouped[unit] = grouped
 
         def quantise_activations(unit):
+            x_words[unit] = x_pool.tile([P, PASSES * E], U32, align_bytes=64, name="x_words")
+            x_scales[unit] = x_pool.tile([P, PASSES * E], U8, align_bytes=64, name="x_scales")
             nc.vector.quantize_mx(
-                out=x_words[:, unit, :].bitcast(FP8X4),
-                scales=x_scales[:, unit, :],
-                in_=x_grouped[unit][:],
+                out=x_words[unit][:].bitcast(FP8X4), scales=x_scales[unit][:], in_=x_grouped[unit][:]
             )
 
         first_accs = {}
         h_grouped = {}
 
-        def first_passes(unit):
-            weight = 1 + unit if unit <= T else 0
-            words, scales = w1_words[weight], w1_scales[weight]
-            first_accs[unit] = []
-            for q in range(PASSES):
+        def first_passes(unit, qs=(0, 1)):
+            w = weight_of_unit[unit]
+            for q in qs:
                 for b in range(E_BLOCKS):
                     acc = psum.tile([P, BANK], F32, tag="bank")
                     for j in range(PACK):
-                        m_cols = slice(j * SLOT_COLS + q * P, j * SLOT_COLS + (q + 1) * P)
+                        m_cols = slice((q * PACK + j) * P, (q * PACK + j + 1) * P)
                         for g in range(PASSES):
                             e_cols = slice(g * E + b * P, g * E + (b + 1) * P)
                             nc.tensor.matmul_mx(
                                 out=acc[:, j * P : (j + 1) * P],
-                                lhsT=words[:, g, m_cols].bitcast(FP8X4),
-                                lhsT_scale=scales[:, g, m_cols],
-                                rhs=x_words[:, unit, e_cols].bitcast(FP8X4),
-                                rhs_scale=x_scales[:, unit, e_cols],
+                                lhsT=w1_words[w][:, g, m_cols].bitcast(FP8X4),
+                                lhsT_scale=w1_scales[w][:, g, m_cols],
+                                rhs=x_words[unit][:, e_cols].bitcast(FP8X4),
+                                rhs_scale=x_scales[unit][:, e_cols],
                                 start=(g == 0),
                                 stop=(g == PASSES - 1),
                             )
-                    first_accs[unit].append(acc)
+                    first_accs[unit, b, q] = acc
 
-        def first_out(unit):
-            grouped = act_pool.tile([P, PASSES * E_BLOCKS, P, PACK], BF16, align_bytes=64, tag="h_grouped", bufs=3)
-            for a, acc in enumerate(first_accs[unit]):
-                interleaved = acc[:].rearrange("p (j r) -> p r j", j=PACK)
+        def first_out(unit, blocks=((0, 0), (1, 0), (0, 1), (1, 1))):
+            if unit not in h_grouped:
+                h_grouped[unit] = act_pool.tile(
+                    [P, E_BLOCKS, PASSES, P, PACK], BF16, align_bytes=64, name="h_grouped"
+                )
+            for b, q in blocks:
+                interleaved = first_accs[unit, b, q][:].rearrange("p (j r) -> p r j", j=PACK)
                 if unit > T:
-                    nc.scalar.copy(out=grouped[:, a], in_=interleaved)
+                    nc.scalar.copy(out=h_grouped[unit][:, b, q], in_=interleaved)
                 else:
-                    bias = first_bias[:, unit * PASSES + a // E_BLOCKS, :]
+                    bias = first_bias[:, unit * PASSES + q, :]
                     nc.vector.tensor_tensor(
-                        out=grouped[:, a],
+                        out=h_grouped[unit][:, b, q],
                         in0=interleaved,
                         in1=bias.unsqueeze(1).to_broadcast([P, P, PACK]),
                         op=ADD,
                     )
-            h_grouped[unit] = grouped
 
-        def quantise_hidden(unit):
+        def quantise_hidden(unit, first=0, last=E_BLOCKS):
+            cols = slice(first * PASSES * P, last * PASSES * P)
             nc.vector.quantize_mx(
-                out=h_words[:, unit, :].bitcast(FP8X4),
-                scales=h_scales[:, unit, :],
-                in_=h_grouped[unit][:].rearrange("p a r j -> p (a r j)"),
+                out=h_words[:, unit, cols].bitcast(FP8X4),
+                scales=h_scales[:, unit, cols],
+                in_=h_grouped[unit][:, first:last].rearrange("p b q r j -> p (b q r j)"),
             )
 
-        def second_passes(index, accs, passes=(0, 1)):
-            h, position = divmod(index - FIRST_CHUNKS, STREAMS)
-            s = SECOND_ORDER[position]
-            for b in range(E_BLOCKS):
-                for t in range(T):
-                    for q in passes:
-                        unit = 0 if s == 0 else 1 + (s - 1) * T + t
-                        e_cols = slice((q * E_BLOCKS + b) * P, (q * E_BLOCKS + b + 1) * P)
-                        nc.tensor.matmul_mx(
-                            out=accs[b * T + t][:],
-                            lhsT=h_words[:, unit, e_cols].bitcast(FP8X4),
-                            lhsT_scale=h_scales[:, unit, e_cols],
-                            rhs=w2_words[:, h, s * PASSES + q, :].bitcast(FP8X4),
-                            rhs_scale=w2_scales[:, h, s * PASSES + q, :],
-                            start=(position == 0 and q == 0),
-                            stop=(position == STREAMS - 1 and q == PASSES - 1),
-                        )
+        def open_banks(directions):
+            return {
+                (b, t): psum.tile([P, BANK], F32, tag="bank", name="acc2") for t in directions for b in range(E_BLOCKS)
+            }
 
-        def open_banks():
-            return [psum.tile([P, BANK], F32, tag="bank", name="acc2") for i in range(E_BLOCKS * T)]
-
-        def finish(h, accs):
-            n_cols = slice(h * BANK, (h + 1) * BANK)
-            for b in range(E_BLOCKS):
-                for t in range(T):
-                    result = result_pool.tile([P, BANK], F32)
-                    nc.vector.tensor_tensor(
-                        out=result[:], in0=accs[b * T + t][:], in1=bk1_all[:, n_cols], op=ADD
+        def second_passes(h, s, banks, passes=(0, 1)):
+            for (b, t), acc in banks.items():
+                unit = 0 if s == 0 else 1 + (s - 1) * T + t
+                for q in passes:
+                    e_cols = slice((b * PASSES + q) * P, (b * PASSES + q + 1) * P)
+                    nc.tensor.matmul_mx(
+                        out=acc[:],
+                        lhsT=h_words[:, unit, e_cols].bitcast(FP8X4),
+                        lhsT_scale=h_scales[:, unit, e_cols],
+                        rhs=w2_words[:, h, s * PASSES + q, :].bitcast(FP8X4),
+                        rhs_scale=w2_scales[:, h, s * PASSES + q, :],
+                        start=(s == 0 and q == 0),
+                        stop=(s == 1 and q == PASSES - 1),
                     )
-                    nc.scalar.activation(out=result[:], in_=result[:], func=SILU)
-                    nc.sync.dma_start(out=out[b * P : (b + 1) * P, t, n_cols], in_=result[:])
 
-        load_next_chunk()
-        load_next_chunk()
-        for t in range(T):
-            load_activations(1 + T + t)
-        load_activations(0)
-        load_next_chunk()
+        def finish(h, banks):
+            n_cols = slice(h * BANK, (h + 1) * BANK)
+            for (b, t), acc in banks.items():
+                result = result_pool.tile([P, BANK], F32)
+                nc.vector.tensor_tensor(out=result[:], in0=acc[:], in1=bk1_all[:, n_cols], op=ADD)
+                nc.scalar.activation(out=result[:], in_=result[:], func=SILU)
+                nc.sync.dma_start(out=out[b * P : (b + 1) * P, t, n_cols], in_=result[:])
 
-        for phase in range(FIRST_WEIGHTS + 1):
-            arriving = phase - 1
-            complete = phase - 2
-            exy_out = T + phase - 1
-            if 1 <= phase < FIRST_WEIGHTS:
-                w1_words[phase] = first_w_pool.tile([P, PASSES, C], U32, align_bytes=64, name="w1_words")
-                w1_scales[phase] = first_w_pool.tile([P, PASSES, C], U8, align_bytes=64, name="w1_scales")
+        def first_weight_tiles(w):
+            w1_words[w] = first_w_pool.tile([P, PASSES, C], U32, align_bytes=64, name="w1_words")
+            w1_scales[w] = first_w_pool.tile([P, PASSES, C], U8, align_bytes=64, name="w1_scales")
 
-            regroup(2 * phase)
-            if phase < T:
-                load_activations(1 + phase)
-            if phase > 0:
-                quantise_chunk(2 * phase - 1)
-            if phase == 1:
-                for t in range(T):
-                    transpose_activations(1 + T + t)
-                bias_cols = psum.tile([P, PACK, P], BF16, tag="bank")
-                for j in range(PACK):
-                    nc.tensor.transpose(bias_cols[:, j, :], sorted_bias[:, j, :], ident_bf16[:])
-                nc.vector.tensor_copy(
-                    out=first_bias[:], in_=bias_cols[:, :, 0:n_bias_rows].rearrange("p j r -> p r j")
-                )
-            if 0 <= arriving <= T:
-                transpose_activations(arriving)
-            if complete >= 0:
-                first_passes(complete)
-            if 2 <= phase <= 1 + T:
-                first_out(exy_out)
+        kx, ky, exy = 0, (1, 2, 3), (4, 5, 6)
 
-            regroup(2 * phase + 1)
-            quantise_chunk(2 * phase)
-            if phase == 1:
-                for t in range(T):
-                    quantise_activations(1 + T + t)
-            if 0 <= arriving <= T:
-                quantise_activations(arriving)
-            if complete >= 0:
-                first_out(complete)
-                quantise_hidden(complete)
-            if 2 <= phase <= 1 + T:
-                quantise_hidden(exy_out)
-            if 1 <= phase <= T:
-                first_passes(T + phase)
+        load_chunk()
+        load_chunk()
+        load_activations(exy[0])
+        load_chunk()
+        load_activations(exy[1])
+        load_chunk()
+        load_activations(kx)
 
-        for h in range(n_halves):
+        regroup(0)
+        load_chunk()
+        load_activations(exy[2])
+        regroup(1)
+        load_chunk()
+        quantise_chunk(0)
+        transpose_activations(exy[0])
+        load_activations(ky[0])
+
+        first_weight_tiles(1)
+        regroup(2)
+        load_chunk()
+        quantise_chunk(1)
+        quantise_activations(exy[0])
+        transpose_activations(exy[1])
+        load_activations(ky[1])
+        bias_cols = psum.tile([P, PACK, P], BF16, tag="bank")
+        for j in range(PACK):
+            nc.tensor.transpose(bias_cols[:, j, :], sorted_bias[:, j, :], ident_bf16[:])
+        nc.vector.tensor_copy(out=first_bias[:], in_=bias_cols[:, :, 0:n_bias_rows].rearrange("p j r -> p r j"))
+        first_passes(exy[0])
+        regroup(3)
+        load_chunk()
+        quantise_chunk(2)
+        quantise_activations(exy[1])
+        transpose_activations(kx)
+        load_activations(ky[2])
+
+        first_weight_tiles(2)
+        regroup(4)
+        load_chunk()
+        quantise_chunk(3)
+        first_out(exy[0])
+        quantise_activations(kx)
+        first_passes(exy[1])
+        transpose_activations(exy[2])
+        first_passes(kx)
+        regroup(5)
+        load_chunk()
+        quantise_chunk(4)
+        quantise_hidden(exy[0])
+        first_out(kx)
+        first_out(exy[1])
+        quantise_activations(exy[2])
+        transpose_activations(ky[0])
+
+        regroup(6)
+        load_chunk()
+        quantise_chunk(5)
+        quantise_activations(ky[0])
+        quantise_hidden(kx)
+        quantise_hidden(exy[1])
+        first_passes(exy[2])
+        first_passes(ky[0])
+        for h in range(HALVES):
             cols = slice(h * BANK, (h + 1) * BANK)
             spread = psum.tile([P, BANK], F32, tag="bank")
             nc.tensor.matmul(out=spread[:], lhsT=ones[:], rhs=bk1_row[:, cols], start=True, stop=True)
             nc.scalar.copy(out=bk1_all[:, cols], in_=spread[:])
+        regroup(7)
+        load_chunk()
+        quantise_chunk(6)
+        first_out(ky[0])
+        first_out(exy[2])
+        transpose_activations(ky[1])
+        regroup(8)
+        load_chunk()
+        quantise_chunk(7)
+        quantise_hidden(ky[0])
+        quantise_hidden(exy[2])
+        quantise_activations(ky[1])
+        banks = open_banks((0,))
+        second_passes(0, 0, banks)
+        second_passes(0, 2, banks)
 
-        accs = open_banks()
-        second_passes(FIRST_CHUNKS, accs)
-        for index in range(FIRST_CHUNKS + 2, n_chunks):
-            regroup(index)
-            quantise_chunk(index - 1)
-            if index - 1 == FIRST_CHUNKS + STREAMS:
-                finish(0, accs)
-                accs = open_banks()
-            second_passes(index - 1, accs)
+        first_weight_tiles(3)
+        regroup(9)
+        load_chunk()
+        quantise_chunk(8)
+        second_passes(0, 1, banks)
+        transpose_activations(ky[2])
+        next_banks = open_banks((1,))
+        second_passes(0, 0, next_banks)
+        second_passes(0, 2, next_banks)
+        regroup(10)
+        load_chunk()
+        quantise_chunk(9)
+        finish(0, banks)
+        quantise_activations(ky[2])
+
+        regroup(11)
+        load_chunk()
+        quantise_chunk(10)
+        first_passes(ky[1])
+        regroup(12)
+        quantise_chunk(11)
+        first_out(ky[1])
+        quantise_hidden(ky[1])
+        second_passes(0, 1, next_banks)
+        banks = open_banks(range(T))
+        second_passes(1, 0, banks)
+
+        first_weight_tiles(4)
+        regroup(13)
+        quantise_chunk(12)
+        finish(0, next_banks)
+        second_passes(1, 2, banks)
+        regroup(14)
+        quantise_chunk(13)
+
+        regroup(15)
+        quantise_chunk(14)
         for q in range(PASSES):
-            quantise_chunk(n_chunks - 1, (q,))
-            second_passes(n_chunks - 1, accs, (q,))
-        finish(1, accs)
+            first_passes(ky[2], (q,))
+            quantise_chunk(15, (q,))
+            first_out(ky[2], ((0, q), (1, q)))
+        early = {key: acc for key, acc in banks.items() if key[1] < T - 1}
+        late = {key: acc for key, acc in banks.items() if key[1] == T - 1}
+        second_passes(1, 1, early)
+        last_banks = open_banks((T - 1,))
+        second_passes(0, 0, last_banks)
+        second_passes(0, 2, last_banks)
+        quantise_hidden(ky[2])
+        finish(1, early)
+        second_passes(0, 1, last_banks)
+        second_passes(1, 1, late)
+        finish(0, last_banks)
+        finish(1, late)

@@ -9,7 +9,6 @@ U32 = mybir.dt.uint32
 U8 = mybir.dt.uint8
 FP8X4 = mybir.dt.float8_e4m3fn_x4
 ADD = mybir.AluOpType.add
-MULT = mybir.AluOpType.mult
 SILU = mybir.ActivationFunctionType.Silu
 
 P = 128
@@ -28,7 +27,7 @@ UNITS = 1 + T + T
 HALF = BANK
 SECOND_ORDER = (0, 2, 1)
 COPY_RUN = 8
-VECTOR_COLS = (576, 576, 560, 560, 672, 672, 400, 400, 400, 512, 512, 320, 320, 384, 384, 256)
+VECTOR_COLS = (576, 576, 560, 560, 672, 672, 416, 416, 416, 480, 480, 288, 288, 352, 352, 256)
 RAW_BUFS = 6
 
 FLOPS = 2 * 2 * UNITS * E * C * C
@@ -56,27 +55,18 @@ def tile_comformerconvedgelayer_pa_kernel(
         first_w_pool = ctx.enter_context(tc.tile_pool(name="first_w", bufs=2))
         x_pool = ctx.enter_context(tc.tile_pool(name="x", bufs=3))
         act_pool = ctx.enter_context(tc.tile_pool(name="act", bufs=3))
-        result_pool = ctx.enter_context(tc.tile_pool(name="result", bufs=6))
+        result_pool = ctx.enter_context(tc.tile_pool(name="result", bufs=8))
         psum = ctx.enter_context(tc.psum_pool(name="psum", bufs=8))
 
         warm = consts.tile([P, 1], F32)
         nc.vector.memset(warm[:], 0.0)
         nc.scalar.activation(out=warm[:], in_=warm[:], func=SILU)
 
-        bias_rows = consts.tile([n_bias_rows, K_PASS], BF16)
+        bias_rows = consts.tile([P, K_PASS], BF16)
+        nc.gpsimd.memset(bias_rows[:], 0.0)
         nc.scalar.dma_start(out=bias_rows[0:PASSES, :], in_=bk.rearrange("(q c) -> q c", q=PASSES))
         nc.scalar.dma_start(
             out=bias_rows[PASSES:n_bias_rows, :], in_=bke.rearrange("t (q c) -> (t q) c", q=PASSES)
-        )
-        sorted_bias = consts.tile([P, PACK, P], BF16)
-        nc.gpsimd.memset(sorted_bias[:], 0.0)
-        nc.gpsimd.tensor_scalar(
-            out=sorted_bias[0:n_bias_rows, :, :],
-            in0=bias_rows[:].rearrange("r (p j) -> r j p", j=PACK),
-            scalar1=1.0,
-            scalar2=0.0,
-            op0=MULT,
-            op1=ADD,
         )
         bk1_row = consts.tile([P, C], BF16)
         nc.vector.memset(bk1_row[:], 0.0)
@@ -89,7 +79,7 @@ def tile_comformerconvedgelayer_pa_kernel(
         ident_bf16 = consts.tile([P, P], BF16)
         make_identity(nc, ident_bf16[:])
         first_bias = consts.tile([P, n_bias_rows, PACK], F32)
-        bk1_all = consts.tile([P, C], F32)
+        bk1_all = consts.tile([P, C], BF16)
 
         h_words = keep.tile([P, UNITS, PASSES * E], U32, align_bytes=64)
         h_scales = keep.tile([P, UNITS, PASSES * E], U8, align_bytes=64)
@@ -274,11 +264,17 @@ def tile_comformerconvedgelayer_pa_kernel(
                         stop=(s == 1 and q == PASSES - 1),
                     )
 
-        def finish(h, banks):
+        def add_bk1(h, banks):
             n_cols = slice(h * BANK, (h + 1) * BANK)
-            for (b, t), acc in banks.items():
-                result = result_pool.tile([P, BANK], F32)
-                nc.vector.tensor_tensor(out=result[:], in0=acc[:], in1=bk1_all[:, n_cols], op=ADD)
+            sums = {}
+            for key, acc in banks.items():
+                sums[key] = result_pool.tile([P, BANK], F32, name="result")
+                nc.vector.tensor_tensor(out=sums[key][:], in0=acc[:], in1=bk1_all[:, n_cols], op=ADD)
+            return sums
+
+        def store(h, sums):
+            n_cols = slice(h * BANK, (h + 1) * BANK)
+            for (b, t), result in sums.items():
                 nc.scalar.activation(out=result[:], in_=result[:], func=SILU)
                 nc.sync.dma_start(out=out[b * P : (b + 1) * P, t, n_cols], in_=result[:])
 
@@ -314,7 +310,7 @@ def tile_comformerconvedgelayer_pa_kernel(
         load_activations(ky[1])
         bias_cols = psum.tile([P, PACK, P], BF16, tag="bank")
         for j in range(PACK):
-            nc.tensor.transpose(bias_cols[:, j, :], sorted_bias[:, j, :], ident_bf16[:])
+            nc.tensor.transpose(bias_cols[:, j, :], bias_rows[:, j::PACK], ident_bf16[:])
         nc.vector.tensor_copy(out=first_bias[:], in_=bias_cols[:, :, 0:n_bias_rows].rearrange("p j r -> p r j"))
         first_passes(exy[0])
         regroup(3)
@@ -350,11 +346,11 @@ def tile_comformerconvedgelayer_pa_kernel(
         quantise_hidden(exy[1])
         first_passes(exy[2])
         first_passes(ky[0])
+        spread = psum.tile([P, C], BF16, tag="bank")
         for h in range(HALVES):
             cols = slice(h * BANK, (h + 1) * BANK)
-            spread = psum.tile([P, BANK], F32, tag="bank")
-            nc.tensor.matmul(out=spread[:], lhsT=ones[:], rhs=bk1_row[:, cols], start=True, stop=True)
-            nc.scalar.copy(out=bk1_all[:, cols], in_=spread[:])
+            nc.tensor.matmul(out=spread[:, cols], lhsT=ones[:], rhs=bk1_row[:, cols], start=True, stop=True)
+        nc.scalar.copy(out=bk1_all[:], in_=spread[:])
         regroup(7)
         load_chunk()
         quantise_chunk(6)
@@ -383,7 +379,7 @@ def tile_comformerconvedgelayer_pa_kernel(
         regroup(10)
         load_chunk()
         quantise_chunk(9)
-        finish(0, banks)
+        sums = {0: add_bk1(0, banks)}
         quantise_activations(ky[2])
 
         regroup(11)
@@ -401,7 +397,7 @@ def tile_comformerconvedgelayer_pa_kernel(
         first_weight_tiles(4)
         regroup(13)
         quantise_chunk(12)
-        finish(0, next_banks)
+        sums[1] = add_bk1(0, next_banks)
         second_passes(1, 2, banks)
         regroup(14)
         quantise_chunk(13)
@@ -418,9 +414,12 @@ def tile_comformerconvedgelayer_pa_kernel(
         last_banks = open_banks((T - 1,))
         second_passes(0, 0, last_banks)
         second_passes(0, 2, last_banks)
+        store(0, sums[0])
+        store(0, sums[1])
         quantise_hidden(ky[2])
-        finish(1, early)
+        early_sums = add_bk1(1, early)
+        store(1, early_sums)
         second_passes(0, 1, last_banks)
         second_passes(1, 1, late)
-        finish(0, last_banks)
-        finish(1, late)
+        store(0, add_bk1(0, last_banks))
+        store(1, add_bk1(1, late))

@@ -27,8 +27,9 @@ UNITS = 1 + T + T
 HALF = BANK
 SECOND_ORDER = (0, 2, 1)
 COPY_RUN = 8
-VECTOR_COLS = (576, 576, 560, 560, 672, 672, 416, 416, 416, 480, 480, 288, 288, 352, 352, 256)
-RAW_BUFS = 6
+VECTOR_COLS = (576, 576, 560, 560, 672, 672, 416, 416, 416, 480, 480, 288, 288, 288, 352, 352)
+SPLIT_CHUNKS = 2
+RAW_BUFS = 5
 
 FLOPS = 2 * 2 * UNITS * E * C * C
 
@@ -43,9 +44,8 @@ def tile_comformerconvedgelayer_pa_kernel(
     order = [("first", w, g) for w in range(3) for g in range(PASSES)]
     order += [("second", s, 0) for s in SECOND_ORDER]
     order += [("first", 3, g) for g in range(PASSES)]
-    order += [("second", s, 1) for s in SECOND_ORDER[:-1]]
+    order += [("second", s, 1) for s in SECOND_ORDER]
     order += [("first", 4, g) for g in range(PASSES)]
-    order += [("second", SECOND_ORDER[-1], 1)]
     n_chunks = len(order)
     with ExitStack() as ctx:
         consts = ctx.enter_context(tc.tile_pool(name="consts", bufs=1))
@@ -96,17 +96,14 @@ def tile_comformerconvedgelayer_pa_kernel(
         def load_chunk():
             index = len(chunks)
             kind, which, part = order[index]
-            if index == 0:
-                halves = [
-                    consts.tile([P, PACK, HALF], BF16, name="raw_left")[:],
-                    consts.tile([P, PACK, HALF], BF16, name="raw_right")[:],
-                ]
+            if index < SPLIT_CHUNKS:
+                halves = [consts.tile([P, PACK, HALF], BF16, name="raw%d_%d" % (index, q))[:] for q in range(PASSES)]
             else:
                 raw = raw_pool.tile([P, PACK, C], BF16)
                 halves = [raw[:, :, 0:HALF], raw[:, :, HALF:C]]
             if kind == "first":
                 rows = first_weights[which][part * K_PASS : (part + 1) * K_PASS, :].rearrange("(p t) c -> p t c", t=PACK)
-                if index == 0:
+                if index < SPLIT_CHUNKS:
                     nc.sync.dma_start(out=halves[0], in_=rows[:, :, 0:HALF])
                     nc.sync.dma_start(out=halves[1], in_=rows[:, :, HALF:C])
                 else:
@@ -125,7 +122,7 @@ def tile_comformerconvedgelayer_pa_kernel(
             for q in range(PASSES):
                 to = grouped[:, q * HALF : (q + 1) * HALF, :]
                 source = chunks[index][q]
-                cut = v_cols // 2 if index in (0, n_chunks - 1) else min(max(v_cols - q * HALF, 0), HALF)
+                cut = v_cols // 2 if index < SPLIT_CHUNKS or index == n_chunks - 1 else min(max(v_cols - q * HALF, 0), HALF)
                 if kind == "first":
                     to = to.rearrange("p (j m) t -> p m t j", j=PACK)
                     source = source.rearrange("p t (m j) -> p m t j", j=PACK)
@@ -394,32 +391,40 @@ def tile_comformerconvedgelayer_pa_kernel(
         banks = open_banks(range(T))
         second_passes(1, 0, banks)
 
-        first_weight_tiles(4)
         regroup(13)
         quantise_chunk(12)
         sums[1] = add_bk1(0, next_banks)
         second_passes(1, 2, banks)
-        regroup(14)
-        quantise_chunk(13)
-
-        regroup(15)
-        quantise_chunk(14)
-        for q in range(PASSES):
-            first_passes(ky[2], (q,))
-            quantise_chunk(15, (q,))
-            first_out(ky[2], ((0, q), (1, q)))
         early = {key: acc for key, acc in banks.items() if key[1] < T - 1}
         late = {key: acc for key, acc in banks.items() if key[1] == T - 1}
+
+        first_weight_tiles(4)
+        regroup(14)
+        quantise_chunk(13)
         second_passes(1, 1, early)
+        regroup(15)
+        quantise_chunk(14)
+        store(0, sums[0])
+        store(0, sums[1])
+        keys = list(early)
+        store(1, add_bk1(1, {key: early[key] for key in keys[:2]}))
         last_banks = open_banks((T - 1,))
         second_passes(0, 0, last_banks)
         second_passes(0, 2, last_banks)
-        store(0, sums[0])
-        store(0, sums[1])
-        quantise_hidden(ky[2])
-        early_sums = add_bk1(1, early)
-        store(1, early_sums)
-        second_passes(0, 1, last_banks)
-        second_passes(1, 1, late)
-        store(0, add_bk1(0, last_banks))
-        store(1, add_bk1(1, late))
+
+        for q in range(PASSES):
+            quantise_chunk(15, (q,))
+            first_passes(ky[2], (q,))
+        first_out(ky[2], ((0, 0), (1, 0)))
+        for b in range(E_BLOCKS):
+            first_out(ky[2], ((b, 1),))
+            quantise_hidden(ky[2], b, b + 1)
+        store(1, add_bk1(1, {key: early[key] for key in keys[2:]}))
+        for b in range(E_BLOCKS):
+            key = (b, T - 1)
+            second_passes(1, 1, {key: late[key]})
+            second_passes(0, 1, {key: last_banks[key]})
+        for b in range(E_BLOCKS):
+            key = (b, T - 1)
+            store(1, add_bk1(1, {key: late[key]}))
+            store(0, add_bk1(0, {key: last_banks[key]}))

@@ -28,8 +28,7 @@ HALF = BANK
 SECOND_ORDER = (0, 2, 1)
 COPY_RUN = 8
 VECTOR_COLS = (576, 576, 560, 560, 672, 672, 416, 416, 416, 480, 480, 288, 288, 288, 352, 352)
-SPLIT_CHUNKS = 2
-RAW_BUFS = 5
+RAW_BUFS = 6
 
 FLOPS = 2 * 2 * UNITS * E * C * C
 
@@ -96,18 +95,11 @@ def tile_comformerconvedgelayer_pa_kernel(
         def load_chunk():
             index = len(chunks)
             kind, which, part = order[index]
-            if index < SPLIT_CHUNKS:
-                halves = [consts.tile([P, PACK, HALF], BF16, name="raw%d_%d" % (index, q))[:] for q in range(PASSES)]
-            else:
-                raw = raw_pool.tile([P, PACK, C], BF16)
-                halves = [raw[:, :, 0:HALF], raw[:, :, HALF:C]]
+            raw = raw_pool.tile([P, PACK, C], BF16)
+            halves = [raw[:, :, 0:HALF], raw[:, :, HALF:C]]
             if kind == "first":
                 rows = first_weights[which][part * K_PASS : (part + 1) * K_PASS, :].rearrange("(p t) c -> p t c", t=PACK)
-                if index < SPLIT_CHUNKS:
-                    nc.sync.dma_start(out=halves[0], in_=rows[:, :, 0:HALF])
-                    nc.sync.dma_start(out=halves[1], in_=rows[:, :, HALF:C])
-                else:
-                    nc.sync.dma_start(out=raw[:], in_=rows)
+                nc.sync.dma_start(out=raw[:], in_=rows)
             else:
                 for q in range(PASSES):
                     top = (which * PASSES + q) * K_PASS
@@ -122,7 +114,7 @@ def tile_comformerconvedgelayer_pa_kernel(
             for q in range(PASSES):
                 to = grouped[:, q * HALF : (q + 1) * HALF, :]
                 source = chunks[index][q]
-                cut = v_cols // 2 if index < SPLIT_CHUNKS or index == n_chunks - 1 else min(max(v_cols - q * HALF, 0), HALF)
+                cut = v_cols // 2 if index == n_chunks - 1 else min(max(v_cols - q * HALF, 0), HALF)
                 if kind == "first":
                     to = to.rearrange("p (j m) t -> p m t j", j=PACK)
                     source = source.rearrange("p t (m j) -> p m t j", j=PACK)

from contextlib import ExitStack

import concourse.mybir as mybir
from concourse.masks import make_identity

F32 = mybir.dt.float32
BF16 = mybir.dt.bfloat16
U32 = mybir.dt.uint32
U8 = mybir.dt.uint8
FP8X4 = mybir.dt.float8_e4m3fn_x4
ADD = mybir.AluOpType.add
SILU = mybir.ActivationFunctionType.Silu

P = 128
PACK = 4
K_PASS = P * PACK
BANK = 512

E = 256
T = 3
C = 1024
E_BLOCKS = E // P
PASSES = C // K_PASS
HALVES = C // BANK
STREAMS = 3
UNITS = 1 + T + T
HALF = BANK
SECOND_ORDER = (0, 2, 1)
COPY_RUN = 8
VECTOR_COLS = (576, 576, 560, 560, 672, 672, 416, 416, 416, 480, 480, 288, 288, 288, 352, 352)
RAW_BUFS = 6

FLOPS = 2 * 2 * UNITS * E * C * C


def tile_comformerconvedgelayer_pa_kernel(
    tc, edge, edge_nei_len, edge_nei_angle, Wk, bk, Wke, bke, We, Wk1, bk1, out
):
    nc = tc.nc
    n_bias_rows = (1 + T) * PASSES
    first_weights = (We, Wk, Wke[0], Wke[1], Wke[2])
    weight_of_unit = (1, 2, 3, 4, 0, 0, 0)
    order = [("first", w, g) for w in range(3) for g in range(PASSES)]
    order += [("second", s, 0) for s in SECOND_ORDER]
    order += [("first", 3, g) for g in range(PASSES)]
    order += [("second", s, 1) for s in SECOND_ORDER]
    order += [("first", 4, g) for g in range(PASSES)]
    n_chunks = len(order)
    with ExitStack() as ctx:
        consts = ctx.enter_context(tc.tile_pool(name="consts", bufs=1))
        keep = ctx.enter_context(tc.tile_pool(name="keep", bufs=1))
        raw_pool = ctx.enter_context(tc.tile_pool(name="raw", bufs=RAW_BUFS))
        grouped_pool = ctx.enter_context(tc.tile_pool(name="grouped", bufs=3))
        first_w_pool = ctx.enter_context(tc.tile_pool(name="first_w", bufs=2))
        x_pool = ctx.enter_context(tc.tile_pool(name="x", bufs=3))
        act_pool = ctx.enter_context(tc.tile_pool(name="act", bufs=3))
        result_pool = ctx.enter_context(tc.tile_pool(name="result", bufs=8))
        psum = ctx.enter_context(tc.psum_pool(name="psum", bufs=8))

        warm = consts.tile([P, 1], F32)
        nc.vector.memset(warm[:], 0.0)
        nc.scalar.activation(out=warm[:], in_=warm[:], func=SILU)

        bias_rows = consts.tile([P, K_PASS], BF16)
        nc.gpsimd.memset(bias_rows[:], 0.0)
        nc.scalar.dma_start(out=bias_rows[0:PASSES, :], in_=bk.rearrange("(q c) -> q c", q=PASSES))
        nc.scalar.dma_start(
            out=bias_rows[PASSES:n_bias_rows, :], in_=bke.rearrange("t (q c) -> (t q) c", q=PASSES)
        )
        bk1_row = consts.tile([P, C], BF16)
        nc.vector.memset(bk1_row[:], 0.0)
        nc.scalar.dma_start(out=bk1_row[0:1, :], in_=bk1.rearrange("(o c) -> o c", o=1))
        ones = consts.tile([P, P], BF16)
        nc.vector.memset(ones[:], 1.0)

        ident_f32 = consts.tile([P, P], F32)
        make_identity(nc, ident_f32[:])
        ident_bf16 = consts.tile([P, P], BF16)
        make_identity(nc, ident_bf16[:])
        first_bias = consts.tile([P, n_bias_rows, PACK], F32)
        bk1_all = consts.tile([P, C], BF16)

        h_words = keep.tile([P, UNITS, PASSES * E], U32, align_bytes=64)
        h_scales = keep.tile([P, UNITS, PASSES * E], U8, align_bytes=64)
        w2_words = keep.tile([P, HALVES, STREAMS * PASSES, BANK], U32, align_bytes=64)
        w2_scales = keep.tile([P, HALVES, STREAMS * PASSES, BANK], U8, align_bytes=64)
        we_words = keep.tile([P, PASSES, C], U32, align_bytes=64)
        we_scales = keep.tile([P, PASSES, C], U8, align_bytes=64)
        w1_words = {0: we_words}
        w1_scales = {0: we_scales}

        chunks = []
        regrouped = {}

        def load_chunk():
            index = len(chunks)
            kind, which, part = order[index]
            raw = raw_pool.tile([P, PACK, C], BF16)
            halves = [raw[:, :, 0:HALF], raw[:, :, HALF:C]]
            if kind == "first":
                rows = first_weights[which][part * K_PASS : (part + 1) * K_PASS, :].rearrange("(p t) c -> p t c", t=PACK)
                nc.sync.dma_start(out=raw[:], in_=rows)
            else:
                for q in range(PASSES):
                    top = (which * PASSES + q) * K_PASS
                    rows = Wk1[top : top + K_PASS, part * BANK : (part + 1) * BANK]
                    nc.sync.dma_start(out=halves[q], in_=rows.rearrange("(p t) n -> p t n", t=PACK))
            chunks.append(halves)

        def regroup(index):
            kind = order[index][0]
            grouped = grouped_pool.tile([P, C, PACK], BF16, align_bytes=64)
            v_cols = VECTOR_COLS[index]
            for q in range(PASSES):
                to = grouped[:, q * HALF : (q + 1) * HALF, :]
                source = chunks[index][q]
                cut = v_cols // 2 if index == n_chunks - 1 else min(max(v_cols - q * HALF, 0), HALF)
                if kind == "first":
                    to = to.rearrange("p (j m) t -> p m t j", j=PACK)
                    source = source.rearrange("p t (m j) -> p m t j", j=PACK)
                    cut = cut // PACK
                else:
                    to = to.rearrange("p (x b) t -> p x t b", b=COPY_RUN)
                    source = source.rearrange("p t (x b) -> p x t b", b=COPY_RUN)
                    cut = cut // COPY_RUN
                if cut > 0:
                    nc.vector.tensor_copy(out=to[:, 0:cut], in_=source[:, 0:cut])
                if cut < to.shape[1]:
                    nc.scalar.copy(out=to[:, cut:], in_=source[:, cut:])
            regrouped[index] = grouped

        def quantise_chunk(index, halves=(0, 1)):
            kind, which, part = order[index]
            for half in halves:
                cols = slice(half * HALF, (half + 1) * HALF)
                if kind == "first":
                    words, scales = w1_words[which][:, part, cols], w1_scales[which][:, part, cols]
                else:
                    row = which * PASSES + half
                    words, scales = w2_words[:, part, row, :], w2_scales[:, part, row, :]
                nc.vector.quantize_mx(
                    out=words.bitcast(FP8X4),
                    scales=scales,
                    in_=regrouped[index][:, cols, :].rearrange("p c t -> p (c t)"),
                )

        x_rows = {}
        x_grouped = {}
        x_words = {}
        x_scales = {}

        def load_activations(unit):
            if unit == 0:
                source = edge
            elif unit <= T:
                source = edge_nei_len[:, unit - 1, :]
            else:
                source = edge_nei_angle[:, unit - 1 - T, :]
            rows = x_pool.tile([P, E_BLOCKS, C], BF16, tag="x_rows", bufs=4)
            nc.sync.dma_start(out=rows[:], in_=source.rearrange("(b p) k -> p b k", p=P))
            x_rows[unit] = rows

        def transpose_activations(unit):
            grouped = act_pool.tile([P, PASSES * E * PACK], BF16, align_bytes=64, tag="x_grouped")
            grouped_pairs = grouped[:].bitcast(F32).rearrange("p (g r u) -> p g r u", g=PASSES, u=2)
            for b in range(E_BLOCKS):
                pairs = x_rows[unit][:, b, :].bitcast(F32)
                turned = psum.tile([P, BANK], F32, tag="bank")
                for w in range(BANK // P):
                    g, u = divmod(w, 2)
                    nc.tensor.transpose(
                        turned[:, w * P : (w + 1) * P], pairs[:, g * 2 * P + u : (g + 1) * 2 * P : 2], ident_f32[:]
                    )
                nc.scalar.copy(
                    out=grouped_pairs[:, :, b * P : (b + 1) * P, :],
                    in_=turned[:].rearrange("p (g u r) -> p g r u", g=PASSES, u=2),
                )
            x_grouped[unit] = grouped

        def quantise_activations(unit):
            x_words[unit] = x_pool.tile([P, PASSES * E], U32, align_bytes=64, name="x_words")
            x_scales[unit] = x_pool.tile([P, PASSES * E], U8, align_bytes=64, name="x_scales")
            nc.vector.quantize_mx(
                out=x_words[unit][:].bitcast(FP8X4), scales=x_scales[unit][:], in_=x_grouped[unit][:]
            )

        first_accs = {}
        h_grouped = {}

        def first_passes(unit, qs=(0, 1)):
            w = weight_of_unit[unit]
            for q in qs:
                for b in range(E_BLOCKS):
                    acc = psum.tile([P, BANK], F32, tag="bank")
                    for j in range(PACK):
                        m_cols = slice((q * PACK + j) * P, (q * PACK + j + 1) * P)
                        for g in range(PASSES):
                            e_cols = slice(g * E + b * P, g * E + (b + 1) * P)
                            nc.tensor.matmul_mx(
                                out=acc[:, j * P : (j + 1) * P],
                                lhsT=w1_words[w][:, g, m_cols].bitcast(FP8X4),
                                lhsT_scale=w1_scales[w][:, g, m_cols],
                                rhs=x_words[unit][:, e_cols].bitcast(FP8X4),
                                rhs_scale=x_scales[unit][:, e_cols],
                                start=(g == 0),
                                stop=(g == PASSES - 1),
                            )
                    first_accs[unit, b, q] = acc

        def first_out(unit, blocks=((0, 0), (1, 0), (0, 1), (1, 1))):
            if unit not in h_grouped:
                h_grouped[unit] = act_pool.tile(
                    [P, E_BLOCKS, PASSES, P, PACK], BF16, align_bytes=64, name="h_grouped"
                )
            for b, q in blocks:
                interleaved = first_accs[unit, b, q][:].rearrange("p (j r) -> p r j", j=PACK)
                if unit > T:
                    nc.scalar.copy(out=h_grouped[unit][:, b, q], in_=interleaved)
                else:
                    bias = first_bias[:, unit * PASSES + q, :]
                    nc.vector.tensor_tensor(
                        out=h_grouped[unit][:, b, q],
                        in0=interleaved,
                        in1=bias.unsqueeze(1).to_broadcast([P, P, PACK]),
                        op=ADD,
                    )

        def quantise_hidden(unit, first=0, last=E_BLOCKS):
            cols = slice(first * PASSES * P, last * PASSES * P)
            nc.vector.quantize_mx(
                out=h_words[:, unit, cols].bitcast(FP8X4),
                scales=h_scales[:, unit, cols],
                in_=h_grouped[unit][:, first:last].rearrange("p b q r j -> p (b q r j)"),
            )

        def open_banks(directions):
            return {
                (b, t): psum.tile([P, BANK], F32, tag="bank", name="acc2") for t in directions for b in range(E_BLOCKS)
            }

        def second_passes(h, s, banks, passes=(0, 1)):
            for (b, t), acc in banks.items():
                unit = 0 if s == 0 else 1 + (s - 1) * T + t
                for q in passes:
                    e_cols = slice((b * PASSES + q) * P, (b * PASSES + q + 1) * P)
                    nc.tensor.matmul_mx(
                        out=acc[:],
                        lhsT=h_words[:, unit, e_cols].bitcast(FP8X4),
                        lhsT_scale=h_scales[:, unit, e_cols],
                        rhs=w2_words[:, h, s * PASSES + q, :].bitcast(FP8X4),
                        rhs_scale=w2_scales[:, h, s * PASSES + q, :],
                        start=(s == 0 and q == 0),
                        stop=(s == 1 and q == PASSES - 1),
                    )

        def add_bk1(h, banks):
            n_cols = slice(h * BANK, (h + 1) * BANK)
            sums = {}
            for key, acc in banks.items():
                sums[key] = result_pool.tile([P, BANK], F32, name="result")
                nc.vector.tensor_tensor(out=sums[key][:], in0=acc[:], in1=bk1_all[:, n_cols], op=ADD)
            return sums

        def store(h, sums):
            n_cols = slice(h * BANK, (h + 1) * BANK)
            for (b, t), result in sums.items():
                nc.scalar.activation(out=result[:], in_=result[:], func=SILU)
                nc.sync.dma_start(out=out[b * P : (b + 1) * P, t, n_cols], in_=result[:])

        def first_weight_tiles(w):
            w1_words[w] = first_w_pool.tile([P, PASSES, C], U32, align_bytes=64, name="w1_words")
            w1_scales[w] = first_w_pool.tile([P, PASSES, C], U8, align_bytes=64, name="w1_scales")

        kx, ky, exy = 0, (1, 2, 3), (4, 5, 6)

        load_chunk()
        load_chunk()
        load_activations(exy[0])
        load_chunk()
        load_activations(exy[1])
        load_chunk()
        load_activations(kx)

        regroup(0)
        load_chunk()
        load_activations(exy[2])
        regroup(1)
        load_chunk()
        quantise_chunk(0)
        transpose_activations(exy[0])
        load_activations(ky[0])

        first_weight_tiles(1)
        regroup(2)
        load_chunk()
        quantise_chunk(1)
        quantise_activations(exy[0])
        transpose_activations(exy[1])
        load_activations(ky[1])
        bias_cols = psum.tile([P, PACK, P], BF16, tag="bank")
        for j in range(PACK):
            nc.tensor.transpose(bias_cols[:, j, :], bias_rows[:, j::PACK], ident_bf16[:])
        nc.vector.tensor_copy(out=first_bias[:], in_=bias_cols[:, :, 0:n_bias_rows].rearrange("p j r -> p r j"))
        first_passes(exy[0])
        regroup(3)
        load_chunk()
        quantise_chunk(2)
        quantise_activations(exy[1])
        transpose_activations(kx)
        load_activations(ky[2])

        first_weight_tiles(2)
        regroup(4)
        load_chunk()
        quantise_chunk(3)
        first_out(exy[0])
        quantise_activations(kx)
        first_passes(exy[1])
        transpose_activations(exy[2])
        first_passes(kx)
        regroup(5)
        load_chunk()
        quantise_chunk(4)
        quantise_hidden(exy[0])
        first_out(kx)
        first_out(exy[1])
        quantise_activations(exy[2])
        transpose_activations(ky[0])

        regroup(6)
        load_chunk()
        quantise_chunk(5)
        quantise_activations(ky[0])
        quantise_hidden(kx)
        quantise_hidden(exy[1])
        first_passes(exy[2])
        first_passes(ky[0])
        spread = psum.tile([P, C], BF16, tag="bank")
        for h in range(HALVES):
            cols = slice(h * BANK, (h + 1) * BANK)
            nc.tensor.matmul(out=spread[:, cols], lhsT=ones[:], rhs=bk1_row[:, cols], start=True, stop=True)
        nc.scalar.copy(out=bk1_all[:], in_=spread[:])
        regroup(7)
        load_chunk()
        quantise_chunk(6)
        first_out(ky[0])
        first_out(exy[2])
        transpose_activations(ky[1])
        regroup(8)
        load_chunk()
        quantise_chunk(7)
        quantise_hidden(ky[0])
        quantise_hidden(exy[2])
        quantise_activations(ky[1])
        banks = open_banks((0,))
        second_passes(0, 0, banks)
        second_passes(0, 2, banks)

        first_weight_tiles(3)
        regroup(9)
        load_chunk()
        quantise_chunk(8)
        second_passes(0, 1, banks)
        transpose_activations(ky[2])
        next_banks = open_banks((1,))
        second_passes(0, 0, next_banks)
        second_passes(0, 2, next_banks)
        regroup(10)
        load_chunk()
        quantise_chunk(9)
        sums = {0: add_bk1(0, banks)}
        quantise_activations(ky[2])

        regroup(11)
        load_chunk()
        quantise_chunk(10)
        first_passes(ky[1])
        regroup(12)
        quantise_chunk(11)
        first_out(ky[1])
        quantise_hidden(ky[1])
        second_passes(0, 1, next_banks)
        banks = open_banks(range(T))
        second_passes(1, 0, banks)

        regroup(13)
        quantise_chunk(12)
        sums[1] = add_bk1(0, next_banks)
        second_passes(1, 2, banks)
        early = {key: acc for key, acc in banks.items() if key[1] < T - 1}
        late = {key: acc for key, acc in banks.items() if key[1] == T - 1}

        first_weight_tiles(4)
        regroup(14)
        quantise_chunk(13)
        second_passes(1, 1, early)
        regroup(15)
        quantise_chunk(14)
        store(0, sums[0])
        store(0, sums[1])
        keys = list(early)
        store(1, add_bk1(1, {key: early[key] for key in keys[:2]}))
        last_banks = open_banks((T - 1,))
        second_passes(0, 0, last_banks)
        second_passes(0, 2, last_banks)

        for q in range(PASSES):
            quantise_chunk(15, (q,))
            first_passes(ky[2], (q,))
        first_out(ky[2], ((0, 0), (1, 0)))
        for b in range(E_BLOCKS):
            first_out(ky[2], ((b, 1),))
            quantise_hidden(ky[2], b, b + 1)
        store(1, add_bk1(1, {key: early[key] for key in keys[2:]}))
        for b in range(E_BLOCKS):
            key = (b, T - 1)
            second_passes(1, 1, {key: late[key]})
            second_passes(0, 1, {key: last_banks[key]})
        for b in range(E_BLOCKS):
            key = (b, T - 1)
            store(1, add_bk1(1, {key: late[key]}))
            store(0, add_bk1(0, {key: last_banks[key]}))
